import numpy as np
import ml_dtypes


def mxq(x, axis, fmt="e4m3"):
    dtype, down = {"e4m3": (ml_dtypes.float8_e4m3fn, 7), "e5m2": (ml_dtypes.float8_e5m2, 14)}[fmt]
    v = np.moveaxis(np.asarray(x, np.float32).astype(ml_dtypes.bfloat16).astype(np.float64), axis, -1)
    blocks = v.reshape(v.shape[:-1] + (-1, 32))
    amax = np.abs(blocks).max(-1, keepdims=True)
    byte = np.maximum(np.where(amax > 0, np.frexp(amax)[1] - 1 + 127, 0) - down, 1)
    scale = np.exp2(byte - 127.0)
    codes = (blocks / scale).astype(np.float32).astype(dtype).astype(np.float64)
    return np.moveaxis((codes * scale).reshape(v.shape), -1, axis)


WIDE = False


def mx_kscale(k):
    if not WIDE:
        return np.ones(k)
    levels = np.array([10, -10, 5, -5, 0])
    a = np.random.permutation(np.resize(levels, k // 512 * 4)).reshape(k // 512, 4)
    idx = np.arange(k)
    return np.exp2(a[idx // 512, idx % 128 // 32])


BF16 = ml_dtypes.bfloat16


def bf(x):
    return np.asarray(x, np.float32).astype(BF16)


def f64(x):
    return np.asarray(x).astype(np.float64)


B, H, W, C, NH, WS, SH, HID = 2, 32, 16, 512, 16, 16, 7, 2048
HD = C // NH
WW = WS * WS
PT, PL = WS - SH, WS - SH
HP, WP = H + WS, W + WS
NWH, NWW = HP // WS, WP // WS
NWIN = B * NWH * NWW
EPS = 1e-5
ERF_CLIP, ERF_TERMS = 6.0, 100


def erf(z):
    z = np.clip(z, -ERF_CLIP, ERF_CLIP)
    zz = 2.0 * z * z
    term = z.copy()
    total = z.copy()
    for n in range(1, ERF_TERMS):
        term = term * zz / (2.0 * n + 1.0)
        total = total + term
    return 2.0 / np.sqrt(np.pi) * np.exp(-z * z) * total


def gelu(v):
    return 0.5 * v * (1.0 + erf(v / np.sqrt(2.0)))


def layer_norm(x, g, b):
    m = x.mean(-1, keepdims=True)
    v = ((x - m) ** 2).mean(-1, keepdims=True)
    return (x - m) / np.sqrt(v + EPS) * g + b


def setup_inputs():
    r = np.random.standard_normal
    s = mx_kscale(C)
    return {
        "h_pad": bf(r((B, HP, WP, C)) * 0.7),
        "x": bf(r((B, H * W, C))),
        "sw": bf(r((NH, WW, WW)) / np.sqrt(WW)),
        "sb": bf(r((NH, WW)) * 0.3),
        "g2": bf((1.0 + 0.2 * r(C)) * s),
        "b2": bf(0.2 * r(C) * s),
        "w1": bf(r((C, HID)) / np.sqrt(C) / s[:, None]),
        "bb1": bf(r(HID) * 0.3),
    }


def reference(h_pad, x, sw, sb, g2, b2, w1, bb1):
    hw = (f64(h_pad).reshape(B, NWH, WS, NWW, WS, NH, HD)
          .transpose(5, 2, 4, 0, 1, 3, 6)
          .reshape(NH, WW, NWIN * HD))
    m = f64(sw) @ hw + f64(sb)[:, :, None]
    m = (m.reshape(NH, WS, WS, B, NWH, NWW, HD)
          .transpose(3, 4, 1, 5, 2, 0, 6)
          .reshape(B, HP, WP, C))
    m = m[:, PT:PT + H, PL:PL + W, :].reshape(B, H * W, C)
    x1 = f64(x) + m
    h2 = layer_norm(x1, f64(g2), f64(b2))
    a = (mxq(h2, 2, "e4m3") @ mxq(f64(w1), 0, "e4m3")) + f64(bb1)
    return gelu(a)

@@ -1,0 +1,312 @@
+from contextlib import ExitStack
+
+import concourse.mybir as mybir
+from concourse.masks import make_identity
+
+BF16 = mybir.dt.bfloat16
+F32 = mybir.dt.float32
+U32 = mybir.dt.uint32
+U8 = mybir.dt.uint8
+FP8X4 = mybir.dt.float8_e4m3fn_x4
+ACT = mybir.ActivationFunctionType
+ALU = mybir.AluOpType
+
+P = 128
+BATCH = 2
+MAP_ROWS = 32
+MAP_COLS = 16
+CH = 512
+HEADS = 16
+WS = 16
+SHIFT = 7
+HID = 2048
+HEAD_CH = CH // HEADS
+POSITIONS = WS * WS
+PAD = WS - SHIFT
+WINDOWS_DOWN = (MAP_ROWS + WS) // WS
+WINDOWS_ACROSS = (MAP_COLS + WS) // WS
+EPS = 1e-5
+
+TILE_ROWS = P // MAP_COLS
+PARITIES = 2
+TILES = BATCH * MAP_ROWS // TILE_ROWS // PARITIES
+HALVES = 2
+PACK = 4
+HEADS_PER_BANK = 4
+HEADS_PER_TRANSPOSE_BANK = 8
+N_MX = 512
+HID_CHUNKS = HID // N_MX
+
+FLOPS = (
+    2 * HEADS * POSITIONS * POSITIONS * BATCH * WINDOWS_DOWN * WINDOWS_ACROSS * HEAD_CH
+    + 2 * BATCH * MAP_ROWS * MAP_COLS * CH * HID
+)
+
+
+def pieces_by_window(first, count):
+    pieces = []
+    offset = 0
+    while offset < count:
+        window, inside = divmod(first + offset, WS)
+        length = min(count - offset, WS - inside)
+        pieces.append((offset, length, inside, window))
+        offset += length
+    return pieces
+
+
+def tile_swinmlpblock_pa_kernel(tc, h_pad, x, sw, sb, g2, b2, w1, bb1, out):
+    nc = tc.nc
+
+    row_pieces = [pieces_by_window(PAD + TILE_ROWS * parity, TILE_ROWS) for parity in range(PARITIES)]
+    col_pieces = pieces_by_window(PAD, MAP_COLS)
+    patches = [[(rp, cp) for rp in row_pieces[parity] for cp in col_pieces] for parity in range(PARITIES)]
+    parity_order = (1, 0)
+
+    with ExitStack() as stack:
+        const = stack.enter_context(tc.tile_pool(name="const", bufs=1))
+        keep = stack.enter_context(tc.tile_pool(name="keep", bufs=1))
+        stage = stack.enter_context(tc.tile_pool(name="stage", bufs=2))
+        results = stack.enter_context(tc.tile_pool(name="results", bufs=4))
+        flip_banks = stack.enter_context(tc.psum_pool(name="flip_banks", bufs=2))
+        mix_banks = stack.enter_context(tc.psum_pool(name="mix_banks", bufs=3))
+        mx_banks = stack.enter_context(tc.psum_pool(name="mx_banks", bufs=3))
+
+        sw_rows = [keep.tile([P, HEADS, POSITIONS], BF16, name="sw_rows%d" % s) for s in range(PARITIES)]
+        sw_flipped = [
+            keep.tile([P, len(patches[s]), HALVES, HEADS, P], BF16, name="sw_flipped%d" % s)
+            for s in range(PARITIES)
+        ]
+        windows = keep.tile([P, WINDOWS_DOWN, BATCH, WINDOWS_ACROSS, HALVES * CH], BF16)
+        x_tiles = [keep.tile([P, TILES, CH], BF16, name="x_tiles%d" % s) for s in range(PARITIES)]
+        x1 = [keep.tile([P, TILES, CH], F32, name="x1_%d" % s) for s in range(PARITIES)]
+        w1_raw = keep.tile([P, HID_CHUNKS, PACK, N_MX], BF16)
+        w1_codes = keep.tile([P, HID], U32, align_bytes=64)
+        w1_scales = keep.tile([P, HID], U8, align_bytes=64)
+        h2_codes = keep.tile([P, PARITIES, TILES * P], U32, align_bytes=64)
+        h2_scales = keep.tile([P, PARITIES, TILES * P], U8, align_bytes=64)
+        bias_rows = const.tile([P, HID], BF16)
+
+        small_rows = const.tile([P, P], BF16)
+        sb_raw = const.tile([HEADS, POSITIONS], BF16)
+        nc.vector.memset(small_rows[:], 0.0)
+        nc.scalar.dma_start(out=sb_raw[:], in_=sb)
+        nc.scalar.dma_start(out=small_rows[0:PACK, :], in_=g2.rearrange("(t p) -> t p", p=P))
+        nc.scalar.dma_start(out=small_rows[PACK : 2 * PACK, :], in_=b2.rearrange("(t p) -> t p", p=P))
+
+        sw_by_row = sw.rearrange("h i j -> i h j")
+        window_view = h_pad.rearrange(
+            "b (wh r) (ww q e) c -> b wh ww r q (e c)", r=WS, ww=WINDOWS_ACROSS, e=HALVES
+        )
+        x_view = x.flatten_outer_dims().rearrange("(g s p) c -> s p g c", s=PARITIES, p=P)
+        w1_view = w1.rearrange("(t p) n -> p t n", p=P)
+        out_rows = out.flatten_outer_dims()
+
+        def load_sw_rows(parity):
+            for offset, length, inside, window in row_pieces[parity]:
+                for heads in (slice(0, HEADS // 2), slice(HEADS // 2, HEADS)):
+                    nc.sync.dma_start(
+                        out=sw_rows[parity][WS * offset : WS * (offset + length), heads, :],
+                        in_=sw_by_row[WS * inside : WS * (inside + length), heads, :],
+                    )
+
+        def load_window_row(wh):
+            for b in range(BATCH):
+                for ww in range(WINDOWS_ACROSS):
+                    nc.sync.dma_start(out=windows[:, wh, b, ww, :], in_=window_view[b, wh, ww])
+
+        load_sw_rows(1)
+        load_window_row(1)
+        load_window_row(2)
+        nc.sync.dma_start(out=x_tiles[1][:], in_=x_view[1])
+        load_sw_rows(0)
+        load_window_row(0)
+        nc.sync.dma_start(out=x_tiles[0][:], in_=x_view[0])
+        nc.sync.dma_start(out=bias_rows[:], in_=bb1.partition_broadcast(P))
+        for n in range(HID_CHUNKS):
+            nc.sync.dma_start(out=w1_raw[:, n, :, :], in_=w1_view[:, :, N_MX * n : N_MX * (n + 1)])
+
+        ident_bf = const.tile([P, P], BF16)
+        ident_f32 = const.tile([P, P], F32)
+        minus_half = const.tile([P, TILES], F32)
+        make_identity(nc, ident_bf[:])
+        make_identity(nc, ident_f32[:])
+        nc.gpsimd.memset(minus_half[:], -0.5)
+
+        warm = const.tile([P, 1], F32)
+        nc.scalar.activation(out=warm[:], in_=minus_half[:, 0:1], func=ACT.Gelu)
+
+        nc.vector.memset(sw_flipped[1][:].rearrange("q a e h m -> q (a e h m)").bitcast(F32), 0.0)
+        nc.gpsimd.memset(sw_flipped[0][:].rearrange("q a e h m -> q (a e h m)").bitcast(F32), 0.0)
+
+        sb_rows = const.tile([P, PARITIES, P], BF16)
+        nc.vector.memset(sb_rows[:], 0.0)
+        sb_grid = sb_raw[:].rearrange("h (r c) -> h r c", c=WS)
+        for parity in range(PARITIES):
+            slot_grid = sb_rows[0:HEADS, parity, :].rearrange("h (r c) -> h r c", c=MAP_COLS)
+            for (r_off, r_len, r_in, r_win), (c_off, c_len, c_in, c_win) in patches[parity]:
+                nc.vector.tensor_copy(
+                    out=slot_grid[:, r_off : r_off + r_len, c_off : c_off + c_len],
+                    in_=sb_grid[:, r_in : r_in + r_len, c_in : c_in + c_len],
+                )
+
+        pick_head = const.tile([P, HEADS, TILES * HEAD_CH], BF16)
+        nc.vector.tensor_copy(
+            out=pick_head[:], in_=ident_bf[:, 0:HEADS].unsqueeze(2).to_broadcast([P, HEADS, TILES * HEAD_CH])
+        )
+
+        small_flipped = flip_banks.tile([P, HEADS_PER_TRANSPOSE_BANK, P], BF16, tag="flip")
+        nc.tensor.transpose(small_flipped[:, 0, :], small_rows[:], ident_bf[:])
+        gain_bias = const.tile([P, 2 * PACK], F32)
+        nc.vector.tensor_copy(out=gain_bias[:], in_=small_flipped[:, 0, 0 : 2 * PACK])
+
+        def flip_sw(parity):
+            by_half = sw_rows[parity][:].rearrange("i h (q e) -> i h e q", e=HALVES)
+            bank_number = 0
+            for e in range(HALVES):
+                for h0 in range(0, HEADS, HEADS_PER_TRANSPOSE_BANK):
+                    bank = flip_banks.tile([P, HEADS_PER_TRANSPOSE_BANK, P], BF16, tag="flip")
+                    for hh in range(HEADS_PER_TRANSPOSE_BANK):
+                        nc.tensor.transpose(bank[:, hh, :], by_half[:, h0 + hh, e, :], ident_bf[:])
+                    bank_grid = bank[:].rearrange("q h (r c) -> q h r c", c=WS)
+                    for a, ((r_off, r_len, r_in, r_win), (c_off, c_len, c_in, c_win)) in enumerate(patches[parity]):
+                        slot_grid = sw_flipped[parity][
+                            :, a, e, h0 : h0 + HEADS_PER_TRANSPOSE_BANK, :
+                        ].rearrange("q h (r c) -> q h r c", c=MAP_COLS)
+                        dst = slot_grid[:, :, r_off : r_off + r_len, c_off : c_off + c_len]
+                        src = bank_grid[:, :, r_off : r_off + r_len, c_in : c_in + c_len]
+                        if bank_number % 2 == 0:
+                            nc.vector.tensor_copy(out=dst, in_=src)
+                        else:
+                            nc.scalar.copy(out=dst, in_=src)
+                    bank_number += 1
+
+        windows_by_half = windows[:].rearrange("q wh b ww (e c) -> q wh b ww e c", e=HALVES)
+
+        def mix(parity):
+            for h0 in range(0, HEADS, HEADS_PER_BANK):
+                bank = mix_banks.tile([P, HEADS_PER_BANK, TILES * HEAD_CH], F32)
+                for hh in range(HEADS_PER_BANK):
+                    h = h0 + hh
+                    nc.tensor.matmul(
+                        bank[:, hh, :],
+                        lhsT=sb_rows[:, parity, :],
+                        rhs=pick_head[:, h, :],
+                        start=True,
+                        stop=False,
+                    )
+                    last = (len(patches[parity]) - 1, HALVES - 1)
+                    for a, ((r_off, r_len, r_in, r_win), (c_off, c_len, c_in, c_win)) in enumerate(patches[parity]):
+                        for e in range(HALVES):
+                            nc.tensor.matmul(
+                                bank[:, hh, :].rearrange("p (b u d) -> p b u d", b=BATCH, d=HEAD_CH),
+                                lhsT=sw_flipped[parity][:, a, e, h, :],
+                                rhs=windows_by_half[
+                                    :, r_win : r_win + 2, :, c_win, e, HEAD_CH * h : HEAD_CH * (h + 1)
+                                ].rearrange("q u b d -> q b u d"),
+                                start=False,
+                                stop=((a, e) == last),
+                            )
+                channels = slice(HEAD_CH * h0, HEAD_CH * (h0 + HEADS_PER_BANK))
+                nc.vector.tensor_tensor(
+                    out=x1[parity][:, :, channels].rearrange("p g (h d) -> p g h d", d=HEAD_CH),
+                    in0=bank[:].rearrange("p h (g d) -> p g h d", d=HEAD_CH),
+                    in1=x_tiles[parity][:, :, channels].rearrange("p g (h d) -> p g h d", d=HEAD_CH),
+                    op=ALU.add,
+                )
+
+        def normalise(parity):
+            stats = stage.tile([P, TILES, 6], F32)
+            mean_var = stage.tile([P, TILES, 2], F32)
+            for g in range(TILES):
+                nc.vector.bn_stats(out=stats[:, g, :], in_=x1[parity][:, g, :])
+            for g in range(TILES):
+                nc.vector.bn_aggr(out=mean_var[:, g, :], in_=stats[:, g, :])
+            var_eps = stage.tile([P, TILES], F32)
+            rstd = stage.tile([P, TILES], F32)
+            nc.vector.tensor_scalar_add(out=var_eps[:], in0=mean_var[:, :, 1], scalar1=EPS)
+            nc.gpsimd.tensor_tensor(out=rstd[:], in0=var_eps[:], in1=minus_half[:], op=ALU.pow)
+            for g in range(TILES):
+                nc.vector.tensor_scalar(
+                    out=x1[parity][:, g, :],
+                    in0=x1[parity][:, g, :],
+                    scalar1=mean_var[:, g, 0:1],
+                    scalar2=rstd[:, g : g + 1],
+                    op0=ALU.subtract,
+                    op1=ALU.mult,
+                )
+
+        def regroup(dst, src):
+            nc.vector.tensor_copy(
+                out=dst.rearrange("p (n i) t -> p n t i", i=4), in_=src.rearrange("p t (n i) -> p n t i", i=4)
+            )
+
+        def quantise_h2(parity):
+            planes = stage.tile([P, PACK, TILES * P], BF16)
+            for t in range(PACK):
+                bank = flip_banks.tile([P, TILES, P], F32, tag="flip")
+                for g in range(TILES):
+                    nc.tensor.transpose(bank[:, g, :], x1[parity][:, g, P * t : P * (t + 1)], ident_f32[:])
+                nc.scalar.activation(
+                    out=planes[:, t, :],
+                    in_=bank[:].rearrange("p g m -> p (g m)"),
+                    func=ACT.Identity,
+                    scale=gain_bias[:, t : t + 1],
+                    bias=gain_bias[:, PACK + t : PACK + t + 1],
+                )
+            h2_words = stage.tile([P, TILES * P, PACK], BF16, align_bytes=64)
+            regroup(h2_words[:], planes[:])
+            nc.vector.quantize_mx(
+                out=h2_codes[:, parity, :].bitcast(FP8X4),
+                scales=h2_scales[:, parity, :],
+                in_=h2_words[:].rearrange("p n t -> p (n t)"),
+            )
+
+        def quantise_w1():
+            w1_words = []
+            for n in range(HID_CHUNKS + 1):
+                if n < HID_CHUNKS:
+                    w1_words.append(stage.tile([P, N_MX, PACK], BF16, align_bytes=64, name="w1_words"))
+                    regroup(w1_words[n][:], w1_raw[:, n, :, :])
+                if n > 0:
+                    columns = slice(N_MX * (n - 1), N_MX * n)
+                    nc.vector.quantize_mx(
+                        out=w1_codes[:, columns].bitcast(FP8X4),
+                        scales=w1_scales[:, columns],
+                        in_=w1_words[n - 1][:].rearrange("p n t -> p (n t)"),
+                    )
+
+        def project(parity):
+            for g in range(TILES):
+                tokens = slice(P * g, P * (g + 1))
+                result = results.tile([P, HID], F32)
+                for n in range(HID_CHUNKS):
+                    columns = slice(N_MX * n, N_MX * (n + 1))
+                    bank = mx_banks.tile([P, N_MX], F32)
+                    nc.tensor.matmul_mx(
+                        out=bank[:],
+                        lhsT=h2_codes[:, parity, tokens].bitcast(FP8X4),
+                        lhsT_scale=h2_scales[:, parity, tokens],
+                        rhs=w1_codes[:, columns].bitcast(FP8X4),
+                        rhs_scale=w1_scales[:, columns],
+                        start=True,
+                        stop=True,
+                    )
+                    nc.vector.tensor_tensor(
+                        out=result[:, columns], in0=bank[:], in1=bias_rows[:, columns], op=ALU.add
+                    )
+                    nc.scalar.activation(out=result[:, columns], in_=result[:, columns], func=ACT.Gelu)
+                first_row = P * (PARITIES * g + parity)
+                nc.sync.dma_start(out=out_rows[first_row : first_row + P, :], in_=result[:])
+
+        first, second = parity_order
+        flip_sw(first)
+        flip_sw(second)
+        mix(first)
+        normalise(first)
+        mix(second)
+        quantise_w1()
+        quantise_h2(first)
+        normalise(second)
+        project(first)
+        quantise_h2(second)
+        project(second)

@@ -33,9 +33,14 @@ TILES = BATCH * MAP_ROWS // TILE_ROWS // PARITIES
 HALVES = 2
 PACK = 4
 HEADS_PER_BANK = 4
-HEADS_PER_TRANSPOSE_BANK = 8
+HEAD_BANKS = HEADS // HEADS_PER_BANK
+BF16_BLOCKS_PER_BANK = 8
 N_MX = 512
 HID_CHUNKS = HID // N_MX
+STATS = 6
+STORE_HALVES = 2
+HALF_HID = HID // STORE_HALVES
+CHUNKS_PER_HALF = HID_CHUNKS // STORE_HALVES
 
 FLOPS = (
     2 * HEADS * POSITIONS * POSITIONS * BATCH * WINDOWS_DOWN * WINDOWS_ACROSS * HEAD_CH
@@ -60,26 +65,25 @@ def tile_swinmlpblock_pa_kernel(tc, h_pad, x, sw, sb, g2, b2, w1, bb1, out):
     row_pieces = [pieces_by_window(PAD + TILE_ROWS * parity, TILE_ROWS) for parity in range(PARITIES)]
     col_pieces = pieces_by_window(PAD, MAP_COLS)
     patches = [[(rp, cp) for rp in row_pieces[parity] for cp in col_pieces] for parity in range(PARITIES)]
-    parity_order = (1, 0)
+    first, second = 1, 0
 
     with ExitStack() as stack:
         const = stack.enter_context(tc.tile_pool(name="const", bufs=1))
         keep = stack.enter_context(tc.tile_pool(name="keep", bufs=1))
         stage = stack.enter_context(tc.tile_pool(name="stage", bufs=2))
-        results = stack.enter_context(tc.tile_pool(name="results", bufs=4))
+        results = stack.enter_context(tc.tile_pool(name="results", bufs=6))
         flip_banks = stack.enter_context(tc.psum_pool(name="flip_banks", bufs=2))
         mix_banks = stack.enter_context(tc.psum_pool(name="mix_banks", bufs=3))
         mx_banks = stack.enter_context(tc.psum_pool(name="mx_banks", bufs=3))
 
         sw_rows = [keep.tile([P, HEADS, POSITIONS], BF16, name="sw_rows%d" % s) for s in range(PARITIES)]
         sw_flipped = [
-            keep.tile([P, len(patches[s]), HALVES, HEADS, P], BF16, name="sw_flipped%d" % s)
-            for s in range(PARITIES)
+            keep.tile([P, len(patches[s]), HEADS, P], F32, name="sw_flipped%d" % s) for s in range(PARITIES)
         ]
         windows = keep.tile([P, WINDOWS_DOWN, BATCH, WINDOWS_ACROSS, HALVES * CH], BF16)
         x_tiles = [keep.tile([P, TILES, CH], BF16, name="x_tiles%d" % s) for s in range(PARITIES)]
         x1 = [keep.tile([P, TILES, CH], F32, name="x1_%d" % s) for s in range(PARITIES)]
-        w1_raw = keep.tile([P, HID_CHUNKS, PACK, N_MX], BF16)
+        w1_raw = keep.tile([P, STORE_HALVES, PACK, HALF_HID], BF16)
         w1_codes = keep.tile([P, HID], U32, align_bytes=64)
         w1_scales = keep.tile([P, HID], U8, align_bytes=64)
         h2_codes = keep.tile([P, PARITIES, TILES * P], U32, align_bytes=64)
@@ -88,10 +92,14 @@ def tile_swinmlpblock_pa_kernel(tc, h_pad, x, sw, sb, g2, b2, w1, bb1, out):
 
         small_rows = const.tile([P, P], BF16)
         sb_raw = const.tile([HEADS, POSITIONS], BF16)
+        bias_first_row = 2 * PACK
         nc.vector.memset(small_rows[:], 0.0)
-        nc.scalar.dma_start(out=sb_raw[:], in_=sb)
         nc.scalar.dma_start(out=small_rows[0:PACK, :], in_=g2.rearrange("(t p) -> t p", p=P))
         nc.scalar.dma_start(out=small_rows[PACK : 2 * PACK, :], in_=b2.rearrange("(t p) -> t p", p=P))
+        nc.scalar.dma_start(
+            out=small_rows[bias_first_row : bias_first_row + HID // P, :], in_=bb1.rearrange("(m p) -> m p", p=P)
+        )
+        nc.scalar.dma_start(out=sb_raw[:], in_=sb)
 
         sw_by_row = sw.rearrange("h i j -> i h j")
         window_view = h_pad.rearrange(
@@ -114,16 +122,15 @@ def tile_swinmlpblock_pa_kernel(tc, h_pad, x, sw, sb, g2, b2, w1, bb1, out):
                 for ww in range(WINDOWS_ACROSS):
                     nc.sync.dma_start(out=windows[:, wh, b, ww, :], in_=window_view[b, wh, ww])
 
-        load_sw_rows(1)
+        load_sw_rows(first)
         load_window_row(1)
         load_window_row(2)
-        nc.sync.dma_start(out=x_tiles[1][:], in_=x_view[1])
-        load_sw_rows(0)
+        nc.sync.dma_start(out=x_tiles[first][:], in_=x_view[first])
+        load_sw_rows(second)
         load_window_row(0)
-        nc.sync.dma_start(out=x_tiles[0][:], in_=x_view[0])
-        nc.sync.dma_start(out=bias_rows[:], in_=bb1.partition_broadcast(P))
-        for n in range(HID_CHUNKS):
-            nc.sync.dma_start(out=w1_raw[:, n, :, :], in_=w1_view[:, :, N_MX * n : N_MX * (n + 1)])
+        nc.sync.dma_start(out=x_tiles[second][:], in_=x_view[second])
+        for half in range(STORE_HALVES):
+            nc.sync.dma_start(out=w1_raw[:, half, :, :], in_=w1_view[:, :, HALF_HID * half : HALF_HID * (half + 1)])
 
         ident_bf = const.tile([P, P], BF16)
         ident_f32 = const.tile([P, P], F32)
@@ -135,8 +142,8 @@ def tile_swinmlpblock_pa_kernel(tc, h_pad, x, sw, sb, g2, b2, w1, bb1, out):
         warm = const.tile([P, 1], F32)
         nc.scalar.activation(out=warm[:], in_=minus_half[:, 0:1], func=ACT.Gelu)
 
-        nc.vector.memset(sw_flipped[1][:].rearrange("q a e h m -> q (a e h m)").bitcast(F32), 0.0)
-        nc.gpsimd.memset(sw_flipped[0][:].rearrange("q a e h m -> q (a e h m)").bitcast(F32), 0.0)
+        for parity in (first, second):
+            nc.vector.memset(sw_flipped[parity][:].rearrange("q a h m -> q (a h m)"), 0.0)
 
         sb_rows = const.tile([P, PARITIES, P], BF16)
         nc.vector.memset(sb_rows[:], 0.0)
@@ -148,79 +155,84 @@ def tile_swinmlpblock_pa_kernel(tc, h_pad, x, sw, sb, g2, b2, w1, bb1, out):
                     out=slot_grid[:, r_off : r_off + r_len, c_off : c_off + c_len],
                     in_=sb_grid[:, r_in : r_in + r_len, c_in : c_in + c_len],
                 )
-
         pick_head = const.tile([P, HEADS, TILES * HEAD_CH], BF16)
         nc.vector.tensor_copy(
             out=pick_head[:], in_=ident_bf[:, 0:HEADS].unsqueeze(2).to_broadcast([P, HEADS, TILES * HEAD_CH])
         )
 
-        small_flipped = flip_banks.tile([P, HEADS_PER_TRANSPOSE_BANK, P], BF16, tag="flip")
+        small_flipped = flip_banks.tile([P, BF16_BLOCKS_PER_BANK, P], BF16, tag="flip")
         nc.tensor.transpose(small_flipped[:, 0, :], small_rows[:], ident_bf[:])
         gain_bias = const.tile([P, 2 * PACK], F32)
+        bias_columns = const.tile([P, HID // P], BF16)
         nc.vector.tensor_copy(out=gain_bias[:], in_=small_flipped[:, 0, 0 : 2 * PACK])
+        nc.vector.tensor_copy(
+            out=bias_columns[:], in_=small_flipped[:, 0, bias_first_row : bias_first_row + HID // P]
+        )
+        for m0 in range(0, HID // P, BF16_BLOCKS_PER_BANK):
+            bank = flip_banks.tile([P, BF16_BLOCKS_PER_BANK, P], BF16, tag="flip")
+            for mm in range(BF16_BLOCKS_PER_BANK):
+                nc.tensor.transpose(
+                    bank[:, mm, :], bias_columns[:, m0 + mm : m0 + mm + 1].to_broadcast([P, P]), ident_bf[:]
+                )
+            nc.vector.tensor_copy(
+                out=bias_rows[:, P * m0 : P * (m0 + BF16_BLOCKS_PER_BANK)], in_=bank[:].rearrange("p m i -> p (m i)")
+            )
 
         def flip_sw(parity):
-            by_half = sw_rows[parity][:].rearrange("i h (q e) -> i h e q", e=HALVES)
-            bank_number = 0
-            for e in range(HALVES):
-                for h0 in range(0, HEADS, HEADS_PER_TRANSPOSE_BANK):
-                    bank = flip_banks.tile([P, HEADS_PER_TRANSPOSE_BANK, P], BF16, tag="flip")
-                    for hh in range(HEADS_PER_TRANSPOSE_BANK):
-                        nc.tensor.transpose(bank[:, hh, :], by_half[:, h0 + hh, e, :], ident_bf[:])
-                    bank_grid = bank[:].rearrange("q h (r c) -> q h r c", c=WS)
-                    for a, ((r_off, r_len, r_in, r_win), (c_off, c_len, c_in, c_win)) in enumerate(patches[parity]):
-                        slot_grid = sw_flipped[parity][
-                            :, a, e, h0 : h0 + HEADS_PER_TRANSPOSE_BANK, :
-                        ].rearrange("q h (r c) -> q h r c", c=MAP_COLS)
-                        dst = slot_grid[:, :, r_off : r_off + r_len, c_off : c_off + c_len]
-                        src = bank_grid[:, :, r_off : r_off + r_len, c_in : c_in + c_len]
-                        if bank_number % 2 == 0:
-                            nc.vector.tensor_copy(out=dst, in_=src)
-                        else:
-                            nc.scalar.copy(out=dst, in_=src)
-                    bank_number += 1
+            sw_words = sw_rows[parity][:].bitcast(F32)
+            flipped_halves = sw_flipped[parity][:].bitcast(BF16)
+            for h0 in range(0, HEADS, HEADS_PER_BANK):
+                bank = flip_banks.tile([P, HEADS_PER_BANK, P], F32, tag="flip")
+                for hh in range(HEADS_PER_BANK):
+                    nc.tensor.transpose(bank[:, hh, :], sw_words[:, h0 + hh, :], ident_f32[:])
+                bank_grid = bank[:].bitcast(BF16).rearrange("q h (r ce) -> q h r ce", ce=WS * HALVES)
+                for a, ((r_off, r_len, r_in, r_win), (c_off, c_len, c_in, c_win)) in enumerate(patches[parity]):
+                    slot_grid = flipped_halves[:, a, h0 : h0 + HEADS_PER_BANK, :].rearrange(
+                        "q h (r ce) -> q h r ce", ce=MAP_COLS * HALVES
+                    )
+                    nc.scalar.copy(
+                        out=slot_grid[:, :, r_off : r_off + r_len, HALVES * c_off : HALVES * (c_off + c_len)],
+                        in_=bank_grid[:, :, r_off : r_off + r_len, HALVES * c_in : HALVES * (c_in + c_len)],
+                    )
 
         windows_by_half = windows[:].rearrange("q wh b ww (e c) -> q wh b ww e c", e=HALVES)
+        stats = [keep.tile([P, TILES, HEAD_BANKS, STATS], F32, name="stats%d" % s) for s in range(PARITIES)]
 
-        def mix(parity):
-            for h0 in range(0, HEADS, HEADS_PER_BANK):
+        def mix(parity, banks):
+            by_half = sw_flipped[parity][:].bitcast(BF16).rearrange("q a h (m e) -> q a h e m", e=HALVES)
+            for k in banks:
                 bank = mix_banks.tile([P, HEADS_PER_BANK, TILES * HEAD_CH], F32)
                 for hh in range(HEADS_PER_BANK):
-                    h = h0 + hh
+                    h = HEADS_PER_BANK * k + hh
                     nc.tensor.matmul(
-                        bank[:, hh, :],
-                        lhsT=sb_rows[:, parity, :],
-                        rhs=pick_head[:, h, :],
-                        start=True,
-                        stop=False,
+                        bank[:, hh, :], lhsT=sb_rows[:, parity, :], rhs=pick_head[:, h, :], start=True, stop=False
                     )
                     last = (len(patches[parity]) - 1, HALVES - 1)
                     for a, ((r_off, r_len, r_in, r_win), (c_off, c_len, c_in, c_win)) in enumerate(patches[parity]):
                         for e in range(HALVES):
                             nc.tensor.matmul(
                                 bank[:, hh, :].rearrange("p (b u d) -> p b u d", b=BATCH, d=HEAD_CH),
-                                lhsT=sw_flipped[parity][:, a, e, h, :],
+                                lhsT=by_half[:, a, h, e, :],
                                 rhs=windows_by_half[
                                     :, r_win : r_win + 2, :, c_win, e, HEAD_CH * h : HEAD_CH * (h + 1)
                                 ].rearrange("q u b d -> q b u d"),
                                 start=False,
                                 stop=((a, e) == last),
                             )
-                channels = slice(HEAD_CH * h0, HEAD_CH * (h0 + HEADS_PER_BANK))
+                channels = slice(P * k, P * (k + 1))
                 nc.vector.tensor_tensor(
                     out=x1[parity][:, :, channels].rearrange("p g (h d) -> p g h d", d=HEAD_CH),
                     in0=bank[:].rearrange("p h (g d) -> p g h d", d=HEAD_CH),
                     in1=x_tiles[parity][:, :, channels].rearrange("p g (h d) -> p g h d", d=HEAD_CH),
                     op=ALU.add,
                 )
+                for g in range(TILES):
+                    nc.vector.bn_stats(out=stats[parity][:, g, k, :], in_=x1[parity][:, g, channels])
 
         def normalise(parity):
-            stats = stage.tile([P, TILES, 6], F32)
             mean_var = stage.tile([P, TILES, 2], F32)
             for g in range(TILES):
-                nc.vector.bn_stats(out=stats[:, g, :], in_=x1[parity][:, g, :])
-            for g in range(TILES):
-                nc.vector.bn_aggr(out=mean_var[:, g, :], in_=stats[:, g, :])
+                nc.vector.bn_aggr(out=mean_var[:, g, :], in_=stats[parity][:, g, :, :].rearrange("p k s -> p (k s)"))
             var_eps = stage.tile([P, TILES], F32)
             rstd = stage.tile([P, TILES], F32)
             nc.vector.tensor_scalar_add(out=var_eps[:], in0=mean_var[:, :, 1], scalar1=EPS)
@@ -235,52 +247,61 @@ def tile_swinmlpblock_pa_kernel(tc, h_pad, x, sw, sb, g2, b2, w1, bb1, out):
                     op1=ALU.mult,
                 )
 
-        def regroup(dst, src):
-            nc.vector.tensor_copy(
-                out=dst.rearrange("p (n i) t -> p n t i", i=4), in_=src.rearrange("p t (n i) -> p n t i", i=4)
-            )
+        def regroup(copy, dst, src):
+            copy(out=dst.rearrange("p (n i) t -> p n t i", i=4), in_=src.rearrange("p t (n i) -> p n t i", i=4))
 
-        def quantise_h2(parity):
-            planes = stage.tile([P, PACK, TILES * P], BF16)
+        planes = [keep.tile([P, PACK, TILES * P], BF16, name="planes%d" % s) for s in range(PARITIES)]
+
+        def flip_h2(parity):
             for t in range(PACK):
                 bank = flip_banks.tile([P, TILES, P], F32, tag="flip")
                 for g in range(TILES):
                     nc.tensor.transpose(bank[:, g, :], x1[parity][:, g, P * t : P * (t + 1)], ident_f32[:])
                 nc.scalar.activation(
-                    out=planes[:, t, :],
+                    out=planes[parity][:, t, :],
                     in_=bank[:].rearrange("p g m -> p (g m)"),
                     func=ACT.Identity,
                     scale=gain_bias[:, t : t + 1],
                     bias=gain_bias[:, PACK + t : PACK + t + 1],
                 )
-            h2_words = stage.tile([P, TILES * P, PACK], BF16, align_bytes=64)
-            regroup(h2_words[:], planes[:])
-            nc.vector.quantize_mx(
-                out=h2_codes[:, parity, :].bitcast(FP8X4),
-                scales=h2_scales[:, parity, :],
-                in_=h2_words[:].rearrange("p n t -> p (n t)"),
-            )
 
-        def quantise_w1():
-            w1_words = []
-            for n in range(HID_CHUNKS + 1):
-                if n < HID_CHUNKS:
-                    w1_words.append(stage.tile([P, N_MX, PACK], BF16, align_bytes=64, name="w1_words"))
-                    regroup(w1_words[n][:], w1_raw[:, n, :, :])
-                if n > 0:
-                    columns = slice(N_MX * (n - 1), N_MX * n)
+        def quantise_h2(parity):
+            h2_words = stage.tile([P, TILES, P, PACK], BF16, align_bytes=64)
+            for g in range(TILES + 1):
+                if g < TILES:
+                    regroup(nc.vector.tensor_copy, h2_words[:, g, :, :], planes[parity][:, :, P * g : P * (g + 1)])
+                if g > 0:
+                    tokens = slice(P * (g - 1), P * g)
                     nc.vector.quantize_mx(
-                        out=w1_codes[:, columns].bitcast(FP8X4),
-                        scales=w1_scales[:, columns],
-                        in_=w1_words[n - 1][:].rearrange("p n t -> p (n t)"),
+                        out=h2_codes[:, parity, tokens].bitcast(FP8X4),
+                        scales=h2_scales[:, parity, tokens],
+                        in_=h2_words[:, g - 1, :, :].rearrange("p n t -> p (n t)"),
                     )
 
-        def project(parity):
-            for g in range(TILES):
-                tokens = slice(P * g, P * (g + 1))
-                result = results.tile([P, HID], F32)
-                for n in range(HID_CHUNKS):
-                    columns = slice(N_MX * n, N_MX * (n + 1))
+        w1_words = keep.tile([P, HID_CHUNKS, N_MX, PACK], BF16, align_bytes=64)
+
+        def regroup_w1(copy, chunks):
+            for n in chunks:
+                half, inside = divmod(n, CHUNKS_PER_HALF)
+                regroup(copy, w1_words[:, n, :, :], w1_raw[:, half, :, N_MX * inside : N_MX * (inside + 1)])
+
+        def quantise_w1():
+            for n in range(HID_CHUNKS):
+                columns = slice(N_MX * n, N_MX * (n + 1))
+                nc.vector.quantize_mx(
+                    out=w1_codes[:, columns].bitcast(FP8X4),
+                    scales=w1_scales[:, columns],
+                    in_=w1_words[:, n, :, :].rearrange("p n t -> p (n t)"),
+                )
+
+        def project(parity, g):
+            tokens = slice(P * g, P * (g + 1))
+            first_row = P * (PARITIES * g + parity)
+            for half in range(STORE_HALVES):
+                result = results.tile([P, HALF_HID], F32)
+                for inside in range(CHUNKS_PER_HALF):
+                    columns = slice(HALF_HID * half + N_MX * inside, HALF_HID * half + N_MX * (inside + 1))
+                    here = slice(N_MX * inside, N_MX * (inside + 1))
                     bank = mx_banks.tile([P, N_MX], F32)
                     nc.tensor.matmul_mx(
                         out=bank[:],
@@ -291,22 +312,29 @@ def tile_swinmlpblock_pa_kernel(tc, h_pad, x, sw, sb, g2, b2, w1, bb1, out):
                         start=True,
                         stop=True,
                     )
-                    nc.vector.tensor_tensor(
-                        out=result[:, columns], in0=bank[:], in1=bias_rows[:, columns], op=ALU.add
-                    )
-                    nc.scalar.activation(out=result[:, columns], in_=result[:, columns], func=ACT.Gelu)
-                first_row = P * (PARITIES * g + parity)
-                nc.sync.dma_start(out=out_rows[first_row : first_row + P, :], in_=result[:])
+                    nc.vector.tensor_tensor(out=result[:, here], in0=bank[:], in1=bias_rows[:, columns], op=ALU.add)
+                    nc.scalar.activation(out=result[:, here], in_=result[:, here], func=ACT.Gelu)
+                nc.sync.dma_start(
+                    out=out_rows[first_row : first_row + P, HALF_HID * half : HALF_HID * (half + 1)], in_=result[:]
+                )
 
-        first, second = parity_order
         flip_sw(first)
+        mix(first, range(HEAD_BANKS))
         flip_sw(second)
-        mix(first)
         normalise(first)
-        mix(second)
+        mix(second, range(0, HEAD_BANKS // 2))
+        regroup_w1(nc.scalar.copy, range(0, HID_CHUNKS // 2))
+        flip_h2(first)
+        regroup_w1(nc.vector.tensor_copy, range(HID_CHUNKS // 2, HID_CHUNKS))
         quantise_w1()
         quantise_h2(first)
+        mix(second, range(HEAD_BANKS // 2, HEAD_BANKS))
+        project(first, 0)
         normalise(second)
-        project(first)
+        flip_h2(second)
+        project(first, 1)
         quantise_h2(second)
-        project(second)
+        project(first, 2)
+        project(first, 3)
+        for g in range(TILES):
+            project(second, g)

@@ -38,6 +38,7 @@ BF16_BLOCKS_PER_BANK = 8
 N_MX = 512
 HID_CHUNKS = HID // N_MX
 STATS = 6
+PAIR = 2
 STORE_HALVES = 2
 HALF_HID = HID // STORE_HALVES
 CHUNKS_PER_HALF = HID_CHUNKS // STORE_HALVES
@@ -71,7 +72,7 @@ def tile_swinmlpblock_pa_kernel(tc, h_pad, x, sw, sb, g2, b2, w1, bb1, out):
         const = stack.enter_context(tc.tile_pool(name="const", bufs=1))
         keep = stack.enter_context(tc.tile_pool(name="keep", bufs=1))
         stage = stack.enter_context(tc.tile_pool(name="stage", bufs=2))
-        results = stack.enter_context(tc.tile_pool(name="results", bufs=6))
+        results = stack.enter_context(tc.tile_pool(name="results", bufs=10))
         flip_banks = stack.enter_context(tc.psum_pool(name="flip_banks", bufs=2))
         mix_banks = stack.enter_context(tc.psum_pool(name="mix_banks", bufs=3))
         mx_banks = stack.enter_context(tc.psum_pool(name="mx_banks", bufs=3))
@@ -93,13 +94,13 @@ def tile_swinmlpblock_pa_kernel(tc, h_pad, x, sw, sb, g2, b2, w1, bb1, out):
         small_rows = const.tile([P, P], BF16)
         sb_raw = const.tile([HEADS, POSITIONS], BF16)
         bias_first_row = 2 * PACK
+        nc.sync.dma_start(out=sb_raw[:], in_=sb)
         nc.vector.memset(small_rows[:], 0.0)
         nc.scalar.dma_start(out=small_rows[0:PACK, :], in_=g2.rearrange("(t p) -> t p", p=P))
         nc.scalar.dma_start(out=small_rows[PACK : 2 * PACK, :], in_=b2.rearrange("(t p) -> t p", p=P))
         nc.scalar.dma_start(
             out=small_rows[bias_first_row : bias_first_row + HID // P, :], in_=bb1.rearrange("(m p) -> m p", p=P)
         )
-        nc.scalar.dma_start(out=sb_raw[:], in_=sb)
 
         sw_by_row = sw.rearrange("h i j -> i h j")
         window_view = h_pad.rearrange(
@@ -111,23 +112,23 @@ def tile_swinmlpblock_pa_kernel(tc, h_pad, x, sw, sb, g2, b2, w1, bb1, out):
 
         def load_sw_rows(parity):
             for offset, length, inside, window in row_pieces[parity]:
-                for heads in (slice(0, HEADS // 2), slice(HEADS // 2, HEADS)):
+                for h0 in range(0, HEADS, HEADS_PER_BANK):
                     nc.sync.dma_start(
-                        out=sw_rows[parity][WS * offset : WS * (offset + length), heads, :],
-                        in_=sw_by_row[WS * inside : WS * (inside + length), heads, :],
+                        out=sw_rows[parity][WS * offset : WS * (offset + length), h0 : h0 + HEADS_PER_BANK, :],
+                        in_=sw_by_row[WS * inside : WS * (inside + length), h0 : h0 + HEADS_PER_BANK, :],
                     )
 
-        def load_window_row(wh):
-            for b in range(BATCH):
-                for ww in range(WINDOWS_ACROSS):
-                    nc.sync.dma_start(out=windows[:, wh, b, ww, :], in_=window_view[b, wh, ww])
+        def load_window_rows(rows):
+            for ww in range(WINDOWS_ACROSS):
+                for wh in rows:
+                    for b in range(BATCH):
+                        nc.sync.dma_start(out=windows[:, wh, b, ww, :], in_=window_view[b, wh, ww])
 
         load_sw_rows(first)
-        load_window_row(1)
-        load_window_row(2)
+        load_window_rows((1, 2))
         nc.sync.dma_start(out=x_tiles[first][:], in_=x_view[first])
         load_sw_rows(second)
-        load_window_row(0)
+        load_window_rows((0,))
         nc.sync.dma_start(out=x_tiles[second][:], in_=x_view[second])
         for half in range(STORE_HALVES):
             nc.sync.dma_start(out=w1_raw[:, half, :, :], in_=w1_view[:, :, HALF_HID * half : HALF_HID * (half + 1)])
@@ -135,14 +136,14 @@ def tile_swinmlpblock_pa_kernel(tc, h_pad, x, sw, sb, g2, b2, w1, bb1, out):
         ident_bf = const.tile([P, P], BF16)
         ident_f32 = const.tile([P, P], F32)
         minus_half = const.tile([P, TILES], F32)
-        make_identity(nc, ident_bf[:])
         make_identity(nc, ident_f32[:])
+        make_identity(nc, ident_bf[:])
         nc.gpsimd.memset(minus_half[:], -0.5)
 
         warm = const.tile([P, 1], F32)
         nc.scalar.activation(out=warm[:], in_=minus_half[:, 0:1], func=ACT.Gelu)
 
-        for parity in (first, second):
+        def clear_sw_flipped(parity):
             nc.vector.memset(sw_flipped[parity][:].rearrange("q a h m -> q (a h m)"), 0.0)
 
         sb_rows = const.tile([P, PARITIES, P], BF16)
@@ -151,32 +152,37 @@ def tile_swinmlpblock_pa_kernel(tc, h_pad, x, sw, sb, g2, b2, w1, bb1, out):
         for parity in range(PARITIES):
             slot_grid = sb_rows[0:HEADS, parity, :].rearrange("h (r c) -> h r c", c=MAP_COLS)
             for (r_off, r_len, r_in, r_win), (c_off, c_len, c_in, c_win) in patches[parity]:
-                nc.vector.tensor_copy(
+                nc.scalar.copy(
                     out=slot_grid[:, r_off : r_off + r_len, c_off : c_off + c_len],
                     in_=sb_grid[:, r_in : r_in + r_len, c_in : c_in + c_len],
                 )
         pick_head = const.tile([P, HEADS, TILES * HEAD_CH], BF16)
-        nc.vector.tensor_copy(
+        nc.scalar.copy(
             out=pick_head[:], in_=ident_bf[:, 0:HEADS].unsqueeze(2).to_broadcast([P, HEADS, TILES * HEAD_CH])
         )
 
-        small_flipped = flip_banks.tile([P, BF16_BLOCKS_PER_BANK, P], BF16, tag="flip")
-        nc.tensor.transpose(small_flipped[:, 0, :], small_rows[:], ident_bf[:])
+        clear_sw_flipped(first)
+
         gain_bias = const.tile([P, 2 * PACK], F32)
         bias_columns = const.tile([P, HID // P], BF16)
-        nc.vector.tensor_copy(out=gain_bias[:], in_=small_flipped[:, 0, 0 : 2 * PACK])
-        nc.vector.tensor_copy(
-            out=bias_columns[:], in_=small_flipped[:, 0, bias_first_row : bias_first_row + HID // P]
-        )
-        for m0 in range(0, HID // P, BF16_BLOCKS_PER_BANK):
-            bank = flip_banks.tile([P, BF16_BLOCKS_PER_BANK, P], BF16, tag="flip")
-            for mm in range(BF16_BLOCKS_PER_BANK):
-                nc.tensor.transpose(
-                    bank[:, mm, :], bias_columns[:, m0 + mm : m0 + mm + 1].to_broadcast([P, P]), ident_bf[:]
-                )
+
+        def spread_small_vectors():
+            small_flipped = mx_banks.tile([P, BF16_BLOCKS_PER_BANK, P], BF16, tag="bank")
+            nc.tensor.transpose(small_flipped[:, 0, :], small_rows[:], ident_bf[:])
+            nc.vector.tensor_copy(out=gain_bias[:], in_=small_flipped[:, 0, 0 : 2 * PACK])
             nc.vector.tensor_copy(
-                out=bias_rows[:, P * m0 : P * (m0 + BF16_BLOCKS_PER_BANK)], in_=bank[:].rearrange("p m i -> p (m i)")
+                out=bias_columns[:], in_=small_flipped[:, 0, bias_first_row : bias_first_row + HID // P]
             )
+            for m0 in range(0, HID // P, BF16_BLOCKS_PER_BANK):
+                bank = mx_banks.tile([P, BF16_BLOCKS_PER_BANK, P], BF16, tag="bank")
+                for mm in range(BF16_BLOCKS_PER_BANK):
+                    nc.tensor.transpose(
+                        bank[:, mm, :], bias_columns[:, m0 + mm : m0 + mm + 1].to_broadcast([P, P]), ident_bf[:]
+                    )
+                nc.vector.tensor_copy(
+                    out=bias_rows[:, P * m0 : P * (m0 + BF16_BLOCKS_PER_BANK)],
+                    in_=bank[:].rearrange("p m i -> p (m i)"),
+                )
 
         def flip_sw(parity):
             sw_words = sw_rows[parity][:].bitcast(F32)
@@ -202,13 +208,17 @@ def tile_swinmlpblock_pa_kernel(tc, h_pad, x, sw, sb, g2, b2, w1, bb1, out):
             by_half = sw_flipped[parity][:].bitcast(BF16).rearrange("q a h (m e) -> q a h e m", e=HALVES)
             for k in banks:
                 bank = mix_banks.tile([P, HEADS_PER_BANK, TILES * HEAD_CH], F32)
-                for hh in range(HEADS_PER_BANK):
-                    h = HEADS_PER_BANK * k + hh
-                    nc.tensor.matmul(
-                        bank[:, hh, :], lhsT=sb_rows[:, parity, :], rhs=pick_head[:, h, :], start=True, stop=False
-                    )
-                    last = (len(patches[parity]) - 1, HALVES - 1)
-                    for a, ((r_off, r_len, r_in, r_win), (c_off, c_len, c_in, c_win)) in enumerate(patches[parity]):
+                heads = range(HEADS_PER_BANK * k, HEADS_PER_BANK * (k + 1))
+                nc.tensor.matmul(
+                    bank[:].rearrange("p h n -> p (h n)"),
+                    lhsT=sb_rows[:, parity, :],
+                    rhs=pick_head[:, heads[0] : heads[0] + HEADS_PER_BANK, :].rearrange("k h n -> k (h n)"),
+                    start=True,
+                    stop=False,
+                )
+                last = (len(patches[parity]) - 1, HEADS_PER_BANK - 1, HALVES - 1)
+                for a, ((r_off, r_len, r_in, r_win), (c_off, c_len, c_in, c_win)) in enumerate(patches[parity]):
+                    for hh, h in enumerate(heads):
                         for e in range(HALVES):
                             nc.tensor.matmul(
                                 bank[:, hh, :].rearrange("p (b u d) -> p b u d", b=BATCH, d=HEAD_CH),
@@ -217,7 +227,7 @@ def tile_swinmlpblock_pa_kernel(tc, h_pad, x, sw, sb, g2, b2, w1, bb1, out):
                                     :, r_win : r_win + 2, :, c_win, e, HEAD_CH * h : HEAD_CH * (h + 1)
                                 ].rearrange("q u b d -> q b u d"),
                                 start=False,
-                                stop=((a, e) == last),
+                                stop=((a, hh, e) == last),
                             )
                 channels = slice(P * k, P * (k + 1))
                 nc.vector.tensor_tensor(
@@ -234,17 +244,20 @@ def tile_swinmlpblock_pa_kernel(tc, h_pad, x, sw, sb, g2, b2, w1, bb1, out):
             for g in range(TILES):
                 nc.vector.bn_aggr(out=mean_var[:, g, :], in_=stats[parity][:, g, :, :].rearrange("p k s -> p (k s)"))
             var_eps = stage.tile([P, TILES], F32)
+            minus_mean = stage.tile([P, TILES], F32)
             rstd = stage.tile([P, TILES], F32)
+            shift = stage.tile([P, TILES], F32)
             nc.vector.tensor_scalar_add(out=var_eps[:], in0=mean_var[:, :, 1], scalar1=EPS)
+            nc.vector.tensor_scalar_mul(out=minus_mean[:], in0=mean_var[:, :, 0], scalar1=-1.0)
             nc.gpsimd.tensor_tensor(out=rstd[:], in0=var_eps[:], in1=minus_half[:], op=ALU.pow)
+            nc.gpsimd.tensor_tensor(out=shift[:], in0=minus_mean[:], in1=rstd[:], op=ALU.mult)
             for g in range(TILES):
-                nc.vector.tensor_scalar(
+                nc.scalar.activation(
                     out=x1[parity][:, g, :],
-                    in0=x1[parity][:, g, :],
-                    scalar1=mean_var[:, g, 0:1],
-                    scalar2=rstd[:, g : g + 1],
-                    op0=ALU.subtract,
-                    op1=ALU.mult,
+                    in_=x1[parity][:, g, :],
+                    func=ACT.Identity,
+                    scale=rstd[:, g : g + 1],
+                    bias=shift[:, g : g + 1],
                 )
 
         def regroup(copy, dst, src):
@@ -252,31 +265,36 @@ def tile_swinmlpblock_pa_kernel(tc, h_pad, x, sw, sb, g2, b2, w1, bb1, out):
 
         planes = [keep.tile([P, PACK, TILES * P], BF16, name="planes%d" % s) for s in range(PARITIES)]
 
-        def flip_h2(parity):
-            for t in range(PACK):
-                bank = flip_banks.tile([P, TILES, P], F32, tag="flip")
-                for g in range(TILES):
-                    nc.tensor.transpose(bank[:, g, :], x1[parity][:, g, P * t : P * (t + 1)], ident_f32[:])
-                nc.scalar.activation(
-                    out=planes[parity][:, t, :],
-                    in_=bank[:].rearrange("p g m -> p (g m)"),
-                    func=ACT.Identity,
-                    scale=gain_bias[:, t : t + 1],
-                    bias=gain_bias[:, PACK + t : PACK + t + 1],
-                )
-
-        def quantise_h2(parity):
-            h2_words = stage.tile([P, TILES, P, PACK], BF16, align_bytes=64)
-            for g in range(TILES + 1):
-                if g < TILES:
-                    regroup(nc.vector.tensor_copy, h2_words[:, g, :, :], planes[parity][:, :, P * g : P * (g + 1)])
-                if g > 0:
-                    tokens = slice(P * (g - 1), P * g)
-                    nc.vector.quantize_mx(
-                        out=h2_codes[:, parity, tokens].bitcast(FP8X4),
-                        scales=h2_scales[:, parity, tokens],
-                        in_=h2_words[:, g - 1, :, :].rearrange("p n t -> p (n t)"),
+        def flip_h2(parity, pair):
+            tokens = slice(PAIR * P * pair, PAIR * P * (pair + 1))
+            for t0 in range(0, PACK, PAIR):
+                bank = flip_banks.tile([P, PAIR, PAIR, P], F32, tag="flip")
+                for tt in range(PAIR):
+                    channels = slice(P * (t0 + tt), P * (t0 + tt + 1))
+                    for gg in range(PAIR):
+                        nc.tensor.transpose(bank[:, tt, gg, :], x1[parity][:, PAIR * pair + gg, channels], ident_f32[:])
+                for tt in range(PAIR):
+                    t = t0 + tt
+                    nc.scalar.activation(
+                        out=planes[parity][:, t, tokens],
+                        in_=bank[:, tt, :, :].rearrange("p g m -> p (g m)"),
+                        func=ACT.Identity,
+                        scale=gain_bias[:, t : t + 1],
+                        bias=gain_bias[:, PACK + t : PACK + t + 1],
                     )
+
+        h2_words = [keep.tile([P, TILES, P, PACK], BF16, align_bytes=64, name="h2_words%d" % s) for s in range(PARITIES)]
+
+        def quantise_h2(parity, pair):
+            for g in range(PAIR * pair, PAIR * (pair + 1)):
+                regroup(nc.vector.tensor_copy, h2_words[parity][:, g, :, :], planes[parity][:, :, P * g : P * (g + 1)])
+            for g in range(PAIR * pair, PAIR * (pair + 1)):
+                tokens = slice(P * g, P * (g + 1))
+                nc.vector.quantize_mx(
+                    out=h2_codes[:, parity, tokens].bitcast(FP8X4),
+                    scales=h2_scales[:, parity, tokens],
+                    in_=h2_words[parity][:, g, :, :].rearrange("p n t -> p (n t)"),
+                )
 
         w1_words = keep.tile([P, HID_CHUNKS, N_MX, PACK], BF16, align_bytes=64)
 
@@ -302,7 +320,7 @@ def tile_swinmlpblock_pa_kernel(tc, h_pad, x, sw, sb, g2, b2, w1, bb1, out):
                 for inside in range(CHUNKS_PER_HALF):
                     columns = slice(HALF_HID * half + N_MX * inside, HALF_HID * half + N_MX * (inside + 1))
                     here = slice(N_MX * inside, N_MX * (inside + 1))
-                    bank = mx_banks.tile([P, N_MX], F32)
+                    bank = mx_banks.tile([P, N_MX], F32, tag="bank")
                     nc.tensor.matmul_mx(
                         out=bank[:],
                         lhsT=h2_codes[:, parity, tokens].bitcast(FP8X4),
@@ -319,22 +337,28 @@ def tile_swinmlpblock_pa_kernel(tc, h_pad, x, sw, sb, g2, b2, w1, bb1, out):
                 )
 
         flip_sw(first)
+        clear_sw_flipped(second)
         mix(first, range(HEAD_BANKS))
+        spread_small_vectors()
         flip_sw(second)
         normalise(first)
         mix(second, range(0, HEAD_BANKS // 2))
         regroup_w1(nc.scalar.copy, range(0, HID_CHUNKS // 2))
-        flip_h2(first)
+        flip_h2(first, 0)
+        flip_h2(first, 1)
         regroup_w1(nc.vector.tensor_copy, range(HID_CHUNKS // 2, HID_CHUNKS))
         quantise_w1()
-        quantise_h2(first)
+        quantise_h2(first, 0)
+        quantise_h2(first, 1)
         mix(second, range(HEAD_BANKS // 2, HEAD_BANKS))
         project(first, 0)
         normalise(second)
-        flip_h2(second)
+        flip_h2(second, 0)
         project(first, 1)
-        quantise_h2(second)
+        quantise_h2(second, 0)
+        flip_h2(second, 1)
         project(first, 2)
+        quantise_h2(second, 1)
         project(first, 3)
         for g in range(TILES):
             project(second, g)

@@ -38,6 +38,8 @@ BF16_BLOCKS_PER_BANK = 8
 N_MX = 512
 HID_CHUNKS = HID // N_MX
 STATS = 6
+LEAD = 1
+MIX_STEPS = HEAD_BANKS + LEAD
 PAIR = 2
 STORE_HALVES = 2
 HALF_HID = HID // STORE_HALVES
@@ -65,7 +67,7 @@ def tile_swinmlpblock_pa_kernel(tc, h_pad, x, sw, sb, g2, b2, w1, bb1, out):
 
     row_pieces = [pieces_by_window(PAD + TILE_ROWS * parity, TILE_ROWS) for parity in range(PARITIES)]
     col_pieces = pieces_by_window(PAD, MAP_COLS)
-    patches = [[(rp, cp) for rp in row_pieces[parity] for cp in col_pieces] for parity in range(PARITIES)]
+    patches = [[(rp, cp) for rp in reversed(row_pieces[parity]) for cp in col_pieces] for parity in range(PARITIES)]
     first, second = 1, 0
 
     with ExitStack() as stack:
@@ -111,8 +113,8 @@ def tile_swinmlpblock_pa_kernel(tc, h_pad, x, sw, sb, g2, b2, w1, bb1, out):
         out_rows = out.flatten_outer_dims()
 
         def load_sw_rows(parity):
-            for offset, length, inside, window in row_pieces[parity]:
-                for h0 in range(0, HEADS, HEADS_PER_BANK):
+            for h0 in range(0, HEADS, HEADS_PER_BANK):
+                for offset, length, inside, window in row_pieces[parity]:
                     nc.sync.dma_start(
                         out=sw_rows[parity][WS * offset : WS * (offset + length), h0 : h0 + HEADS_PER_BANK, :],
                         in_=sw_by_row[WS * inside : WS * (inside + length), h0 : h0 + HEADS_PER_BANK, :],
@@ -204,40 +206,55 @@ def tile_swinmlpblock_pa_kernel(tc, h_pad, x, sw, sb, g2, b2, w1, bb1, out):
         windows_by_half = windows[:].rearrange("q wh b ww (e c) -> q wh b ww e c", e=HALVES)
         stats = [keep.tile([P, TILES, HEAD_BANKS, STATS], F32, name="stats%d" % s) for s in range(PARITIES)]
 
-        def mix(parity, banks):
+        open_banks = {}
+
+        def add_patches(parity, k, bank, which):
             by_half = sw_flipped[parity][:].bitcast(BF16).rearrange("q a h (m e) -> q a h e m", e=HALVES)
-            for k in banks:
-                bank = mix_banks.tile([P, HEADS_PER_BANK, TILES * HEAD_CH], F32)
-                heads = range(HEADS_PER_BANK * k, HEADS_PER_BANK * (k + 1))
-                nc.tensor.matmul(
-                    bank[:].rearrange("p h n -> p (h n)"),
-                    lhsT=sb_rows[:, parity, :],
-                    rhs=pick_head[:, heads[0] : heads[0] + HEADS_PER_BANK, :].rearrange("k h n -> k (h n)"),
-                    start=True,
-                    stop=False,
-                )
-                last = (len(patches[parity]) - 1, HEADS_PER_BANK - 1, HALVES - 1)
-                for a, ((r_off, r_len, r_in, r_win), (c_off, c_len, c_in, c_win)) in enumerate(patches[parity]):
-                    for hh, h in enumerate(heads):
-                        for e in range(HALVES):
-                            nc.tensor.matmul(
-                                bank[:, hh, :].rearrange("p (b u d) -> p b u d", b=BATCH, d=HEAD_CH),
-                                lhsT=by_half[:, a, h, e, :],
-                                rhs=windows_by_half[
-                                    :, r_win : r_win + 2, :, c_win, e, HEAD_CH * h : HEAD_CH * (h + 1)
-                                ].rearrange("q u b d -> q b u d"),
-                                start=False,
-                                stop=((a, hh, e) == last),
-                            )
-                channels = slice(P * k, P * (k + 1))
-                nc.vector.tensor_tensor(
-                    out=x1[parity][:, :, channels].rearrange("p g (h d) -> p g h d", d=HEAD_CH),
-                    in0=bank[:].rearrange("p h (g d) -> p g h d", d=HEAD_CH),
-                    in1=x_tiles[parity][:, :, channels].rearrange("p g (h d) -> p g h d", d=HEAD_CH),
-                    op=ALU.add,
-                )
-                for g in range(TILES):
-                    nc.vector.bn_stats(out=stats[parity][:, g, k, :], in_=x1[parity][:, g, channels])
+            last = (len(patches[parity]) - 1, HEADS_PER_BANK - 1, HALVES - 1)
+            for a in which:
+                (r_off, r_len, r_in, r_win), (c_off, c_len, c_in, c_win) = patches[parity][a]
+                for hh in range(HEADS_PER_BANK):
+                    h = HEADS_PER_BANK * k + hh
+                    for e in range(HALVES):
+                        nc.tensor.matmul(
+                            bank[:, hh, :].rearrange("p (b u d) -> p b u d", b=BATCH, d=HEAD_CH),
+                            lhsT=by_half[:, a, h, e, :],
+                            rhs=windows_by_half[
+                                :, r_win : r_win + 2, :, c_win, e, HEAD_CH * h : HEAD_CH * (h + 1)
+                            ].rearrange("q u b d -> q b u d"),
+                            start=False,
+                            stop=((a, hh, e) == last),
+                        )
+
+        def mix(parity, steps):
+            early = len(patches[parity]) // 2
+            for step in steps:
+                if step < HEAD_BANKS:
+                    bank = mix_banks.tile([P, HEADS_PER_BANK, TILES * HEAD_CH], F32)
+                    open_banks[(parity, step)] = bank
+                    nc.tensor.matmul(
+                        bank[:].rearrange("p h n -> p (h n)"),
+                        lhsT=sb_rows[:, parity, :],
+                        rhs=pick_head[:, HEADS_PER_BANK * step : HEADS_PER_BANK * (step + 1), :].rearrange(
+                            "k h n -> k (h n)"
+                        ),
+                        start=True,
+                        stop=False,
+                    )
+                    add_patches(parity, step, bank, range(0, early))
+                if step >= LEAD:
+                    k = step - LEAD
+                    bank = open_banks[(parity, k)]
+                    add_patches(parity, k, bank, range(early, len(patches[parity])))
+                    channels = slice(P * k, P * (k + 1))
+                    nc.vector.tensor_tensor(
+                        out=x1[parity][:, :, channels].rearrange("p g (h d) -> p g h d", d=HEAD_CH),
+                        in0=bank[:].rearrange("p h (g d) -> p g h d", d=HEAD_CH),
+                        in1=x_tiles[parity][:, :, channels].rearrange("p g (h d) -> p g h d", d=HEAD_CH),
+                        op=ALU.add,
+                    )
+                    for g in range(TILES):
+                        nc.vector.bn_stats(out=stats[parity][:, g, k, :], in_=x1[parity][:, g, channels])
 
         def normalise(parity):
             mean_var = stage.tile([P, TILES, 2], F32)
@@ -338,11 +355,11 @@ def tile_swinmlpblock_pa_kernel(tc, h_pad, x, sw, sb, g2, b2, w1, bb1, out):
 
         flip_sw(first)
         clear_sw_flipped(second)
-        mix(first, range(HEAD_BANKS))
+        mix(first, range(MIX_STEPS))
         spread_small_vectors()
         flip_sw(second)
         normalise(first)
-        mix(second, range(0, HEAD_BANKS // 2))
+        mix(second, range(0, MIX_STEPS // 2 + 1))
         regroup_w1(nc.scalar.copy, range(0, HID_CHUNKS // 2))
         flip_h2(first, 0)
         flip_h2(first, 1)
@@ -350,7 +367,7 @@ def tile_swinmlpblock_pa_kernel(tc, h_pad, x, sw, sb, g2, b2, w1, bb1, out):
         quantise_w1()
         quantise_h2(first, 0)
         quantise_h2(first, 1)
-        mix(second, range(HEAD_BANKS // 2, HEAD_BANKS))
+        mix(second, range(MIX_STEPS // 2 + 1, MIX_STEPS))
         project(first, 0)
         normalise(second)
         flip_h2(second, 0)

@@ -145,8 +145,8 @@ def tile_swinmlpblock_pa_kernel(tc, h_pad, x, sw, sb, g2, b2, w1, bb1, out):
         warm = const.tile([P, 1], F32)
         nc.scalar.activation(out=warm[:], in_=minus_half[:, 0:1], func=ACT.Gelu)
 
-        def clear_sw_flipped(parity):
-            nc.vector.memset(sw_flipped[parity][:].rearrange("q a h m -> q (a h m)"), 0.0)
+        def clear_sw_flipped(parity, engine):
+            engine.memset(sw_flipped[parity][:].rearrange("q a h m -> q (a h m)"), 0.0)
 
         sb_rows = const.tile([P, PARITIES, P], BF16)
         nc.vector.memset(sb_rows[:], 0.0)
@@ -163,7 +163,8 @@ def tile_swinmlpblock_pa_kernel(tc, h_pad, x, sw, sb, g2, b2, w1, bb1, out):
             out=pick_head[:], in_=ident_bf[:, 0:HEADS].unsqueeze(2).to_broadcast([P, HEADS, TILES * HEAD_CH])
         )
 
-        clear_sw_flipped(first)
+        clear_sw_flipped(first, nc.vector)
+        clear_sw_flipped(second, nc.gpsimd)
 
         gain_bias = const.tile([P, 2 * PACK], F32)
         bias_columns = const.tile([P, HID // P], BF16)
@@ -261,20 +262,17 @@ def tile_swinmlpblock_pa_kernel(tc, h_pad, x, sw, sb, g2, b2, w1, bb1, out):
             for g in range(TILES):
                 nc.vector.bn_aggr(out=mean_var[:, g, :], in_=stats[parity][:, g, :, :].rearrange("p k s -> p (k s)"))
             var_eps = stage.tile([P, TILES], F32)
-            minus_mean = stage.tile([P, TILES], F32)
             rstd = stage.tile([P, TILES], F32)
-            shift = stage.tile([P, TILES], F32)
             nc.vector.tensor_scalar_add(out=var_eps[:], in0=mean_var[:, :, 1], scalar1=EPS)
-            nc.vector.tensor_scalar_mul(out=minus_mean[:], in0=mean_var[:, :, 0], scalar1=-1.0)
             nc.gpsimd.tensor_tensor(out=rstd[:], in0=var_eps[:], in1=minus_half[:], op=ALU.pow)
-            nc.gpsimd.tensor_tensor(out=shift[:], in0=minus_mean[:], in1=rstd[:], op=ALU.mult)
             for g in range(TILES):
-                nc.scalar.activation(
+                nc.vector.tensor_scalar(
                     out=x1[parity][:, g, :],
-                    in_=x1[parity][:, g, :],
-                    func=ACT.Identity,
-                    scale=rstd[:, g : g + 1],
-                    bias=shift[:, g : g + 1],
+                    in0=x1[parity][:, g, :],
+                    scalar1=mean_var[:, g, 0:1],
+                    scalar2=rstd[:, g : g + 1],
+                    op0=ALU.subtract,
+                    op1=ALU.mult,
                 )
 
         def regroup(copy, dst, src):
@@ -354,7 +352,6 @@ def tile_swinmlpblock_pa_kernel(tc, h_pad, x, sw, sb, g2, b2, w1, bb1, out):
                 )
 
         flip_sw(first)
-        clear_sw_flipped(second)
         mix(first, range(MIX_STEPS))
         spread_small_vectors()
         flip_sw(second)

from contextlib import ExitStack

import concourse.mybir as mybir
from concourse.masks import make_identity

BF16 = mybir.dt.bfloat16
F32 = mybir.dt.float32
U32 = mybir.dt.uint32
U8 = mybir.dt.uint8
FP8X4 = mybir.dt.float8_e4m3fn_x4
ACT = mybir.ActivationFunctionType
ALU = mybir.AluOpType

P = 128
BATCH = 2
MAP_ROWS = 32
MAP_COLS = 16
CH = 512
HEADS = 16
WS = 16
SHIFT = 7
HID = 2048
HEAD_CH = CH // HEADS
POSITIONS = WS * WS
PAD = WS - SHIFT
WINDOWS_DOWN = (MAP_ROWS + WS) // WS
WINDOWS_ACROSS = (MAP_COLS + WS) // WS
EPS = 1e-5

TILE_ROWS = P // MAP_COLS
PARITIES = 2
TILES = BATCH * MAP_ROWS // TILE_ROWS // PARITIES
HALVES = 2
PACK = 4
HEADS_PER_BANK = 4
HEAD_BANKS = HEADS // HEADS_PER_BANK
BF16_BLOCKS_PER_BANK = 8
N_MX = 512
HID_CHUNKS = HID // N_MX
STATS = 6
LEAD = 1
MIX_STEPS = HEAD_BANKS + LEAD
PAIR = 2
STORE_HALVES = 2
HALF_HID = HID // STORE_HALVES
CHUNKS_PER_HALF = HID_CHUNKS // STORE_HALVES

FLOPS = (
    2 * HEADS * POSITIONS * POSITIONS * BATCH * WINDOWS_DOWN * WINDOWS_ACROSS * HEAD_CH
    + 2 * BATCH * MAP_ROWS * MAP_COLS * CH * HID
)


def pieces_by_window(first, count):
    pieces = []
    offset = 0
    while offset < count:
        window, inside = divmod(first + offset, WS)
        length = min(count - offset, WS - inside)
        pieces.append((offset, length, inside, window))
        offset += length
    return pieces


def tile_swinmlpblock_pa_kernel(tc, h_pad, x, sw, sb, g2, b2, w1, bb1, out):
    nc = tc.nc

    row_pieces = [pieces_by_window(PAD + TILE_ROWS * parity, TILE_ROWS) for parity in range(PARITIES)]
    col_pieces = pieces_by_window(PAD, MAP_COLS)
    patches = [[(rp, cp) for rp in reversed(row_pieces[parity]) for cp in col_pieces] for parity in range(PARITIES)]
    first, second = 1, 0

    with ExitStack() as stack:
        const = stack.enter_context(tc.tile_pool(name="const", bufs=1))
        keep = stack.enter_context(tc.tile_pool(name="keep", bufs=1))
        stage = stack.enter_context(tc.tile_pool(name="stage", bufs=2))
        results = stack.enter_context(tc.tile_pool(name="results", bufs=10))
        flip_banks = stack.enter_context(tc.psum_pool(name="flip_banks", bufs=2))
        mix_banks = stack.enter_context(tc.psum_pool(name="mix_banks", bufs=3))
        mx_banks = stack.enter_context(tc.psum_pool(name="mx_banks", bufs=3))

        sw_rows = [keep.tile([P, HEADS, POSITIONS], BF16, name="sw_rows%d" % s) for s in range(PARITIES)]
        sw_flipped = [
            keep.tile([P, len(patches[s]), HEADS, P], F32, name="sw_flipped%d" % s) for s in range(PARITIES)
        ]
        windows = keep.tile([P, WINDOWS_DOWN, BATCH, WINDOWS_ACROSS, HALVES * CH], BF16)
        x_tiles = [keep.tile([P, TILES, CH], BF16, name="x_tiles%d" % s) for s in range(PARITIES)]
        x1 = [keep.tile([P, TILES, CH], F32, name="x1_%d" % s) for s in range(PARITIES)]
        w1_raw = keep.tile([P, STORE_HALVES, PACK, HALF_HID], BF16)
        w1_codes = keep.tile([P, HID], U32, align_bytes=64)
        w1_scales = keep.tile([P, HID], U8, align_bytes=64)
        h2_codes = keep.tile([P, PARITIES, TILES * P], U32, align_bytes=64)
        h2_scales = keep.tile([P, PARITIES, TILES * P], U8, align_bytes=64)
        bias_rows = const.tile([P, HID], BF16)

        small_rows = const.tile([P, P], BF16)
        sb_raw = const.tile([HEADS, POSITIONS], BF16)
        bias_first_row = 2 * PACK
        nc.sync.dma_start(out=sb_raw[:], in_=sb)
        nc.vector.memset(small_rows[:], 0.0)
        nc.scalar.dma_start(out=small_rows[0:PACK, :], in_=g2.rearrange("(t p) -> t p", p=P))
        nc.scalar.dma_start(out=small_rows[PACK : 2 * PACK, :], in_=b2.rearrange("(t p) -> t p", p=P))
        nc.scalar.dma_start(
            out=small_rows[bias_first_row : bias_first_row + HID // P, :], in_=bb1.rearrange("(m p) -> m p", p=P)
        )

        sw_by_row = sw.rearrange("h i j -> i h j")
        window_view = h_pad.rearrange(
            "b (wh r) (ww q e) c -> b wh ww r q (e c)", r=WS, ww=WINDOWS_ACROSS, e=HALVES
        )
        x_view = x.flatten_outer_dims().rearrange("(g s p) c -> s p g c", s=PARITIES, p=P)
        w1_view = w1.rearrange("(t p) n -> p t n", p=P)
        out_rows = out.flatten_outer_dims()

        def load_sw_rows(parity):
            for h0 in range(0, HEADS, HEADS_PER_BANK):
                for offset, length, inside, window in row_pieces[parity]:
                    nc.sync.dma_start(
                        out=sw_rows[parity][WS * offset : WS * (offset + length), h0 : h0 + HEADS_PER_BANK, :],
                        in_=sw_by_row[WS * inside : WS * (inside + length), h0 : h0 + HEADS_PER_BANK, :],
                    )

        def load_window_rows(rows):
            for ww in range(WINDOWS_ACROSS):
                for wh in rows:
                    for b in range(BATCH):
                        nc.sync.dma_start(out=windows[:, wh, b, ww, :], in_=window_view[b, wh, ww])

        load_sw_rows(first)
        load_window_rows((1, 2))
        nc.sync.dma_start(out=x_tiles[first][:], in_=x_view[first])
        load_sw_rows(second)
        load_window_rows((0,))
        nc.sync.dma_start(out=x_tiles[second][:], in_=x_view[second])
        for half in range(STORE_HALVES):
            nc.sync.dma_start(out=w1_raw[:, half, :, :], in_=w1_view[:, :, HALF_HID * half : HALF_HID * (half + 1)])

        ident_bf = const.tile([P, P], BF16)
        ident_f32 = const.tile([P, P], F32)
        minus_half = const.tile([P, TILES], F32)
        make_identity(nc, ident_f32[:])
        make_identity(nc, ident_bf[:])
        nc.gpsimd.memset(minus_half[:], -0.5)

        warm = const.tile([P, 1], F32)
        nc.scalar.activation(out=warm[:], in_=minus_half[:, 0:1], func=ACT.Gelu)

        def clear_sw_flipped(parity, engine):
            engine.memset(sw_flipped[parity][:].rearrange("q a h m -> q (a h m)"), 0.0)

        sb_rows = const.tile([P, PARITIES, P], BF16)
        nc.vector.memset(sb_rows[:], 0.0)
        sb_grid = sb_raw[:].rearrange("h (r c) -> h r c", c=WS)
        for parity in range(PARITIES):
            slot_grid = sb_rows[0:HEADS, parity, :].rearrange("h (r c) -> h r c", c=MAP_COLS)
            for (r_off, r_len, r_in, r_win), (c_off, c_len, c_in, c_win) in patches[parity]:
                nc.scalar.copy(
                    out=slot_grid[:, r_off : r_off + r_len, c_off : c_off + c_len],
                    in_=sb_grid[:, r_in : r_in + r_len, c_in : c_in + c_len],
                )
        pick_head = const.tile([P, HEADS, TILES * HEAD_CH], BF16)
        nc.scalar.copy(
            out=pick_head[:], in_=ident_bf[:, 0:HEADS].unsqueeze(2).to_broadcast([P, HEADS, TILES * HEAD_CH])
        )

        clear_sw_flipped(first, nc.vector)
        clear_sw_flipped(second, nc.gpsimd)

        gain_bias = const.tile([P, 2 * PACK], F32)
        bias_columns = const.tile([P, HID // P], BF16)

        def spread_small_vectors():
            small_flipped = mx_banks.tile([P, BF16_BLOCKS_PER_BANK, P], BF16, tag="bank")
            nc.tensor.transpose(small_flipped[:, 0, :], small_rows[:], ident_bf[:])
            nc.vector.tensor_copy(out=gain_bias[:], in_=small_flipped[:, 0, 0 : 2 * PACK])
            nc.vector.tensor_copy(
                out=bias_columns[:], in_=small_flipped[:, 0, bias_first_row : bias_first_row + HID // P]
            )
            for m0 in range(0, HID // P, BF16_BLOCKS_PER_BANK):
                bank = mx_banks.tile([P, BF16_BLOCKS_PER_BANK, P], BF16, tag="bank")
                for mm in range(BF16_BLOCKS_PER_BANK):
                    nc.tensor.transpose(
                        bank[:, mm, :], bias_columns[:, m0 + mm : m0 + mm + 1].to_broadcast([P, P]), ident_bf[:]
                    )
                nc.vector.tensor_copy(
                    out=bias_rows[:, P * m0 : P * (m0 + BF16_BLOCKS_PER_BANK)],
                    in_=bank[:].rearrange("p m i -> p (m i)"),
                )

        def flip_sw(parity):
            sw_words = sw_rows[parity][:].bitcast(F32)
            flipped_halves = sw_flipped[parity][:].bitcast(BF16)
            for h0 in range(0, HEADS, HEADS_PER_BANK):
                bank = flip_banks.tile([P, HEADS_PER_BANK, P], F32, tag="flip")
                for hh in range(HEADS_PER_BANK):
                    nc.tensor.transpose(bank[:, hh, :], sw_words[:, h0 + hh, :], ident_f32[:])
                bank_grid = bank[:].bitcast(BF16).rearrange("q h (r ce) -> q h r ce", ce=WS * HALVES)
                for a, ((r_off, r_len, r_in, r_win), (c_off, c_len, c_in, c_win)) in enumerate(patches[parity]):
                    slot_grid = flipped_halves[:, a, h0 : h0 + HEADS_PER_BANK, :].rearrange(
                        "q h (r ce) -> q h r ce", ce=MAP_COLS * HALVES
                    )
                    nc.scalar.copy(
                        out=slot_grid[:, :, r_off : r_off + r_len, HALVES * c_off : HALVES * (c_off + c_len)],
                        in_=bank_grid[:, :, r_off : r_off + r_len, HALVES * c_in : HALVES * (c_in + c_len)],
                    )

        windows_by_half = windows[:].rearrange("q wh b ww (e c) -> q wh b ww e c", e=HALVES)
        stats = [keep.tile([P, TILES, HEAD_BANKS, STATS], F32, name="stats%d" % s) for s in range(PARITIES)]

        open_banks = {}

        def add_patches(parity, k, bank, which):
            by_half = sw_flipped[parity][:].bitcast(BF16).rearrange("q a h (m e) -> q a h e m", e=HALVES)
            last = (len(patches[parity]) - 1, HEADS_PER_BANK - 1, HALVES - 1)
            for a in which:
                (r_off, r_len, r_in, r_win), (c_off, c_len, c_in, c_win) = patches[parity][a]
                for hh in range(HEADS_PER_BANK):
                    h = HEADS_PER_BANK * k + hh
                    for e in range(HALVES):
                        nc.tensor.matmul(
                            bank[:, hh, :].rearrange("p (b u d) -> p b u d", b=BATCH, d=HEAD_CH),
                            lhsT=by_half[:, a, h, e, :],
                            rhs=windows_by_half[
                                :, r_win : r_win + 2, :, c_win, e, HEAD_CH * h : HEAD_CH * (h + 1)
                            ].rearrange("q u b d -> q b u d"),
                            start=False,
                            stop=((a, hh, e) == last),
                        )

        def mix(parity, steps):
            early = len(patches[parity]) // 2
            for step in steps:
                if step < HEAD_BANKS:
                    bank = mix_banks.tile([P, HEADS_PER_BANK, TILES * HEAD_CH], F32)
                    open_banks[(parity, step)] = bank
                    nc.tensor.matmul(
                        bank[:].rearrange("p h n -> p (h n)"),
                        lhsT=sb_rows[:, parity, :],
                        rhs=pick_head[:, HEADS_PER_BANK * step : HEADS_PER_BANK * (step + 1), :].rearrange(
                            "k h n -> k (h n)"
                        ),
                        start=True,
                        stop=False,
                    )
                    add_patches(parity, step, bank, range(0, early))
                if step >= LEAD:
                    k = step - LEAD
                    bank = open_banks[(parity, k)]
                    add_patches(parity, k, bank, range(early, len(patches[parity])))
                    channels = slice(P * k, P * (k + 1))
                    nc.vector.tensor_tensor(
                        out=x1[parity][:, :, channels].rearrange("p g (h d) -> p g h d", d=HEAD_CH),
                        in0=bank[:].rearrange("p h (g d) -> p g h d", d=HEAD_CH),
                        in1=x_tiles[parity][:, :, channels].rearrange("p g (h d) -> p g h d", d=HEAD_CH),
                        op=ALU.add,
                    )
                    for g in range(TILES):
                        nc.vector.bn_stats(out=stats[parity][:, g, k, :], in_=x1[parity][:, g, channels])

        def normalise(parity):
            mean_var = stage.tile([P, TILES, 2], F32)
            for g in range(TILES):
                nc.vector.bn_aggr(out=mean_var[:, g, :], in_=stats[parity][:, g, :, :].rearrange("p k s -> p (k s)"))
            var_eps = stage.tile([P, TILES], F32)
            rstd = stage.tile([P, TILES], F32)
            nc.vector.tensor_scalar_add(out=var_eps[:], in0=mean_var[:, :, 1], scalar1=EPS)
            nc.gpsimd.tensor_tensor(out=rstd[:], in0=var_eps[:], in1=minus_half[:], op=ALU.pow)
            for g in range(TILES):
                nc.vector.tensor_scalar(
                    out=x1[parity][:, g, :],
                    in0=x1[parity][:, g, :],
                    scalar1=mean_var[:, g, 0:1],
                    scalar2=rstd[:, g : g + 1],
                    op0=ALU.subtract,
                    op1=ALU.mult,
                )

        def regroup(copy, dst, src):
            copy(out=dst.rearrange("p (n i) t -> p n t i", i=4), in_=src.rearrange("p t (n i) -> p n t i", i=4))

        planes = [keep.tile([P, PACK, TILES * P], BF16, name="planes%d" % s) for s in range(PARITIES)]

        def flip_h2(parity, pair):
            tokens = slice(PAIR * P * pair, PAIR * P * (pair + 1))
            for t0 in range(0, PACK, PAIR):
                bank = flip_banks.tile([P, PAIR, PAIR, P], F32, tag="flip")
                for tt in range(PAIR):
                    channels = slice(P * (t0 + tt), P * (t0 + tt + 1))
                    for gg in range(PAIR):
                        nc.tensor.transpose(bank[:, tt, gg, :], x1[parity][:, PAIR * pair + gg, channels], ident_f32[:])
                for tt in range(PAIR):
                    t = t0 + tt
                    nc.scalar.activation(
                        out=planes[parity][:, t, tokens],
                        in_=bank[:, tt, :, :].rearrange("p g m -> p (g m)"),
                        func=ACT.Identity,
                        scale=gain_bias[:, t : t + 1],
                        bias=gain_bias[:, PACK + t : PACK + t + 1],
                    )

        h2_words = [keep.tile([P, TILES, P, PACK], BF16, align_bytes=64, name="h2_words%d" % s) for s in range(PARITIES)]

        def quantise_h2(parity, pair):
            for g in range(PAIR * pair, PAIR * (pair + 1)):
                regroup(nc.vector.tensor_copy, h2_words[parity][:, g, :, :], planes[parity][:, :, P * g : P * (g + 1)])
            for g in range(PAIR * pair, PAIR * (pair + 1)):
                tokens = slice(P * g, P * (g + 1))
                nc.vector.quantize_mx(
                    out=h2_codes[:, parity, tokens].bitcast(FP8X4),
                    scales=h2_scales[:, parity, tokens],
                    in_=h2_words[parity][:, g, :, :].rearrange("p n t -> p (n t)"),
                )

        w1_words = keep.tile([P, HID_CHUNKS, N_MX, PACK], BF16, align_bytes=64)

        def regroup_w1(copy, chunks):
            for n in chunks:
                half, inside = divmod(n, CHUNKS_PER_HALF)
                regroup(copy, w1_words[:, n, :, :], w1_raw[:, half, :, N_MX * inside : N_MX * (inside + 1)])

        def quantise_w1():
            for n in range(HID_CHUNKS):
                columns = slice(N_MX * n, N_MX * (n + 1))
                nc.vector.quantize_mx(
                    out=w1_codes[:, columns].bitcast(FP8X4),
                    scales=w1_scales[:, columns],
                    in_=w1_words[:, n, :, :].rearrange("p n t -> p (n t)"),
                )

        def project(parity, g):
            tokens = slice(P * g, P * (g + 1))
            first_row = P * (PARITIES * g + parity)
            for half in range(STORE_HALVES):
                result = results.tile([P, HALF_HID], F32)
                for inside in range(CHUNKS_PER_HALF):
                    columns = slice(HALF_HID * half + N_MX * inside, HALF_HID * half + N_MX * (inside + 1))
                    here = slice(N_MX * inside, N_MX * (inside + 1))
                    bank = mx_banks.tile([P, N_MX], F32, tag="bank")
                    nc.tensor.matmul_mx(
                        out=bank[:],
                        lhsT=h2_codes[:, parity, tokens].bitcast(FP8X4),
                        lhsT_scale=h2_scales[:, parity, tokens],
                        rhs=w1_codes[:, columns].bitcast(FP8X4),
                        rhs_scale=w1_scales[:, columns],
                        start=True,
                        stop=True,
                    )
                    nc.vector.tensor_tensor(out=result[:, here], in0=bank[:], in1=bias_rows[:, columns], op=ALU.add)
                    nc.scalar.activation(out=result[:, here], in_=result[:, here], func=ACT.Gelu)
                nc.sync.dma_start(
                    out=out_rows[first_row : first_row + P, HALF_HID * half : HALF_HID * (half + 1)], in_=result[:]
                )

        flip_sw(first)
        mix(first, range(MIX_STEPS))
        spread_small_vectors()
        flip_sw(second)
        normalise(first)
        mix(second, range(0, MIX_STEPS // 2 + 1))
        regroup_w1(nc.scalar.copy, range(0, HID_CHUNKS // 2))
        flip_h2(first, 0)
        flip_h2(first, 1)
        regroup_w1(nc.vector.tensor_copy, range(HID_CHUNKS // 2, HID_CHUNKS))
        quantise_w1()
        quantise_h2(first, 0)
        quantise_h2(first, 1)
        mix(second, range(MIX_STEPS // 2 + 1, MIX_STEPS))
        project(first, 0)
        normalise(second)
        flip_h2(second, 0)
        project(first, 1)
        quantise_h2(second, 0)
        flip_h2(second, 1)
        project(first, 2)
        quantise_h2(second, 1)
        project(first, 3)
        for g in range(TILES):
            project(second, g)
